import numpy as np
import ml_dtypes


def mxq(x, axis, fmt="e4m3"):
    dtype, down = {"e4m3": (ml_dtypes.float8_e4m3fn, 7), "e5m2": (ml_dtypes.float8_e5m2, 14)}[fmt]
    v = np.moveaxis(np.asarray(x, np.float32).astype(ml_dtypes.bfloat16).astype(np.float64), axis, -1)
    blocks = v.reshape(v.shape[:-1] + (-1, 32))
    amax = np.abs(blocks).max(-1, keepdims=True)
    byte = np.maximum(np.where(amax > 0, np.frexp(amax)[1] - 1 + 127, 0) - down, 1)
    scale = np.exp2(byte - 127.0)
    codes = (blocks / scale).astype(np.float32).astype(dtype).astype(np.float64)
    return np.moveaxis((codes * scale).reshape(v.shape), -1, axis)


WIDE = False


def mx_kscale(k):
    if not WIDE:
        return np.ones(k)
    levels = np.array([10, -10, 5, -5, 0])
    if k % 512:
        return np.exp2(np.random.permutation(np.resize(levels, k // 32))).repeat(32)
    a = np.empty((k // 512, 16))
    for p in range(k // 512):
        a[p, :8] = np.random.permutation(np.resize(levels, 8))
        for g in range(8):
            far = levels[np.abs(levels - a[p, g]) >= 10]
            a[p, g + 8] = far[np.random.randint(len(far))]
    return np.exp2(a.ravel()).repeat(32)


BF16 = ml_dtypes.bfloat16


def bf(x):
    return np.asarray(x, np.float32).astype(BF16)


def f64(x):
    return np.asarray(x).astype(np.float64)


B, S, E, H, W = 64, 64, 512, 8, 16


def setup_inputs():
    s = mx_kscale(E)
    t = mx_kscale(2 * E)
    th, tv = t[:E], t[E:]
    return {
        "h_ctx": bf(np.random.standard_normal((B, S, E)) * 0.35 * s),
        "v_ctx": bf(np.random.standard_normal((B, S, E)) * 0.35 * s),
        "h_out_w": bf(np.random.standard_normal((E, E)) * 2.5 / np.sqrt(E) / s[None, :] * th[:, None]),
        "h_out_b": bf(np.random.standard_normal(E) * 0.2 * th),
        "v_out_w": bf(np.random.standard_normal((E, E)) * 2.5 / np.sqrt(E) / s[None, :] * tv[:, None]),
        "v_out_b": bf(np.random.standard_normal(E) * 0.2 * tv),
        "mlp_w1": bf(np.random.standard_normal((E, 2 * E)) / np.sqrt(2 * E) / t[None, :]),
        "mlp_b1": bf(np.random.standard_normal(E) * 0.2),
    }


def reference(h_ctx, v_ctx, h_out_w, h_out_b, v_out_w, v_out_b, mlp_w1, mlp_b1):
    h_out = (mxq(f64(h_ctx), 2, "e4m3") @ mxq(f64(h_out_w), 1, "e4m3").T) + f64(h_out_b)
    v_out = (mxq(f64(v_ctx), 2, "e4m3") @ mxq(f64(v_out_w), 1, "e4m3").T) + f64(v_out_b)
    combined = np.concatenate([h_out, v_out], axis=-1)
    return np.maximum((mxq(combined, 2, "e4m3") @ mxq(f64(mlp_w1), 1, "e4m3").T) + f64(mlp_b1), 0.0)

@@ -1,0 +1,279 @@
+from contextlib import ExitStack
+
+import concourse.mybir as mybir
+from concourse.masks import make_identity
+
+F32 = mybir.dt.float32
+BF16 = mybir.dt.bfloat16
+U32 = mybir.dt.uint32
+U8 = mybir.dt.uint8
+FP8X4 = mybir.dt.float8_e4m3fn_x4
+ACT = mybir.ActivationFunctionType
+ALU = mybir.AluOpType
+
+P = 128
+E = 512
+CHUNK = 512
+N_CHUNKS = 8
+N_UNITS = 2 * N_CHUNKS
+FLOPS = 2 * 4096 * 512 * 512 * 2 + 2 * 4096 * 1024 * 512
+
+PINNED = False
+XT_V_BELOW = 2
+X1_V_BELOW = 2
+RELU_S_FROM = 6
+RELU_S_TILES = 2
+S2_LAG = 2
+
+
+def tile_bispa_pa_t_kernel(
+    tc, h_ctx, v_ctx, h_out_w, h_out_b, v_out_w, v_out_b, mlp_w1, mlp_b1, out
+):
+    nc = tc.nc
+    with ExitStack() as ctx:
+        consts = ctx.enter_context(tc.tile_pool(name="consts", bufs=1))
+        raw = ctx.enter_context(tc.tile_pool(name="raw", bufs=1))
+        wq = ctx.enter_context(tc.tile_pool(name="wq", bufs=1))
+        grp_pool = ctx.enter_context(tc.tile_pool(name="grp", bufs=3))
+        xq = ctx.enter_context(tc.tile_pool(name="xq", bufs=4))
+        pl_pool = ctx.enter_context(tc.tile_pool(name="pl", bufs=3))
+        g2_pool = ctx.enter_context(tc.tile_pool(name="g2", bufs=3))
+        cq = ctx.enter_context(tc.tile_pool(name="cq", bufs=6))
+        ob_pool = ctx.enter_context(tc.tile_pool(name="ob", bufs=4))
+        ps_tp = ctx.enter_context(tc.psum_pool(name="ps", bufs=8))
+        ps_s1 = ps_tp
+        ps_s2 = ps_tp
+        if PINNED:
+            ctx.enter_context(tc.manual_schedule())
+
+        hx = h_ctx.flatten_outer_dims()
+        vx = v_ctx.flatten_outer_dims()
+        of = out.flatten_outer_dims()
+
+        zb = consts.tile([P, E], BF16, name="zb")
+        nc.vector.memset(zb[:], 0.0)
+        zrow = consts.tile([P, E], BF16, name="zrow")
+        nc.vector.memset(zrow[:], 0.0)
+        ones = consts.tile([P, P], BF16, name="ones")
+        nc.vector.memset(ones[:], 1.0)
+        ident = consts.tile([P, P], F32, name="ident")
+        make_identity(nc, ident[:])
+        nc.sync.dma_start(out=zb[0:1, :], in_=h_out_b.rearrange("(o n) -> o n", o=1))
+        nc.sync.dma_start(out=zb[1:2, :], in_=v_out_b.rearrange("(o n) -> o n", o=1))
+        nc.sync.dma_start(out=zrow[0:1, :], in_=mlp_b1.rearrange("(o n) -> o n", o=1))
+
+        def load_proj(w, name):
+            t = raw.tile([P, 4 * E], BF16, name=name)
+            nc.sync.dma_start(
+                out=t[:].rearrange("q (t k) -> q t k", t=4),
+                in_=w.rearrange("(q t) k -> q t k", t=4),
+            )
+            return t
+
+        def load_ctx(x, c, name):
+            t = raw.tile([P, 4 * E], BF16, name=name)
+            nc.sync.dma_start(
+                out=t[:].rearrange("p (a k) -> p a k", a=4),
+                in_=x[c * CHUNK : (c + 1) * CHUNK, :].rearrange("(p a) k -> p a k", a=4),
+            )
+            return t
+
+        ctx_raw = {}
+        hw_raw = load_proj(h_out_w, "hw_raw")
+        ctx_raw[0] = load_ctx(hx, 0, "x0")
+        vw_raw = load_proj(v_out_w, "vw_raw")
+        ctx_raw[1] = load_ctx(vx, 0, "x1")
+        w1_raw = raw.tile([P, 4 * 2 * E], BF16, name="w1_raw")
+        nc.sync.dma_start(
+            out=w1_raw[:].rearrange("p (j k) -> p j k", j=4),
+            in_=mlp_w1.rearrange("(j p) k -> p j k", p=P),
+        )
+        for c in range(1, N_CHUNKS):
+            ctx_raw[2 * c] = load_ctx(hx, c, "x%d" % (2 * c))
+            ctx_raw[2 * c + 1] = load_ctx(vx, c, "x%d" % (2 * c + 1))
+
+        def copy_out(on_vector, dst, src):
+            if on_vector:
+                nc.vector.tensor_copy(out=dst, in_=src)
+            else:
+                nc.scalar.copy(out=dst, in_=src)
+
+        def transpose_quantise(words, row_words, first_word, codes, scales, second_on_vector):
+            grp = grp_pool.tile([P, 4 * E], BF16, align_bytes=64)
+            grp_words = grp[:].bitcast(F32)
+            for half in range(2):
+                bank = ps_tp.tile([P, E], F32, tag="ps")
+                for jj in range(2):
+                    for u in range(2):
+                        start = (2 * half + jj) * row_words + first_word + u
+                        nc.tensor.transpose(
+                            bank[:, u * 256 + jj * P : u * 256 + (jj + 1) * P],
+                            words[:, start : start + 2 * P - 1 : 2],
+                            ident[:],
+                        )
+                copy_out(
+                    second_on_vector and half == 1,
+                    grp_words[:, half * E : (half + 1) * E].rearrange("p (r u) -> p r u", u=2),
+                    bank[:].rearrange("p (u r) -> p r u", u=2),
+                )
+            nc.vector.quantize_mx(out=codes[:].bitcast(FP8X4), scales=scales[:], in_=grp[:])
+
+        def weight_unit(words, row_words, first_word, name, second_on_vector):
+            codes = wq.tile([P, E], U32, name=name + "_c", align_bytes=64)
+            scales = wq.tile([P, E], U8, name=name + "_s", align_bytes=64)
+            transpose_quantise(words, row_words, first_word, codes, scales, second_on_vector)
+            return codes, scales
+
+        state = {}
+
+        def prepare_biases():
+            bank = ps_tp.tile([P, E], F32, tag="ps")
+            zw = zb[:].bitcast(F32)
+            for u in range(2):
+                nc.tensor.transpose(bank[:, u * P : (u + 1) * P], zw[:, u : u + 2 * P - 1 : 2], ident[:])
+            bias8 = consts.tile([P, 8], F32, name="bias8")
+            nc.vector.tensor_copy(
+                out=bias8[:].rearrange("p (s u e) -> p u s e", s=2, u=2),
+                in_=bank[:].bitcast(BF16)[:, 0 : 4 * P].rearrange("p (u x) -> p u x", u=2)[:, :, 0:4].rearrange("p u (s e) -> p u s e", s=2),
+            )
+            state["bias8"] = bias8
+            acc = ps_s2.tile([P, E], F32, tag="ps")
+            nc.tensor.matmul(out=acc[:], lhsT=ones[:], rhs=zrow[:], start=True, stop=True)
+            b1_bc = consts.tile([P, E], F32, name="b1_bc")
+            nc.vector.tensor_copy(out=b1_bc[:], in_=acc[:])
+            state["b1_bc"] = b1_bc
+
+        def tq(j):
+            if j < 0 or j >= N_UNITS:
+                return
+            xc = xq.tile([P, E], U32, align_bytes=64)
+            xs = xq.tile([P, E], U8, align_bytes=64)
+            transpose_quantise(ctx_raw[j][:].bitcast(F32), 256, 0, xc, xs, j < XT_V_BELOW)
+            state["x%d" % j] = (xc, xs)
+
+        def stage1(j):
+            if j < 0 or j >= N_UNITS:
+                return
+            s = j % 2
+            wc, ws = state["w%d" % s]
+            xc, xs = state["x%d" % j]
+            bias8 = state["bias8"]
+            planar = pl_pool.tile([P, 4 * CHUNK], BF16)
+            banks = []
+            for t in range(4):
+                acc1 = ps_s1.tile([P, CHUNK], F32, tag="ps")
+                nc.tensor.matmul_mx(
+                    out=acc1[:],
+                    lhsT=wc[:, t * P : (t + 1) * P].bitcast(FP8X4),
+                    lhsT_scale=ws[:, t * P : (t + 1) * P],
+                    rhs=xc[:].bitcast(FP8X4),
+                    rhs_scale=xs[:],
+                    start=True,
+                    stop=True,
+                )
+                banks.append(acc1)
+            for t in range(4):
+                dst = planar[:, t * CHUNK : (t + 1) * CHUNK]
+                b = bias8[:, 4 * s + t : 4 * s + t + 1]
+                if j < X1_V_BELOW and t % 2 == 1:
+                    nc.vector.tensor_scalar_add(out=dst, in0=banks[t][:], scalar1=b)
+                else:
+                    nc.scalar.activation(out=dst, in_=banks[t][:], func=ACT.Identity, bias=b, scale=1.0)
+            state["p%d" % j] = planar
+
+        def regroup(j):
+            if j < 0 or j >= N_UNITS:
+                return
+            planar = state["p%d" % j]
+            g2 = g2_pool.tile([P, 4 * CHUNK], BF16, align_bytes=64)
+            nc.vector.tensor_copy(
+                out=g2[:].rearrange("p (c i t) -> p c t i", i=4, t=4),
+                in_=planar[:].rearrange("p (t c i) -> p c t i", t=4, i=4),
+            )
+            state["g%d" % j] = g2
+
+        def quantise2(j):
+            if j < 0 or j >= N_UNITS:
+                return
+            cc = cq.tile([P, CHUNK], U32, align_bytes=64)
+            cs = cq.tile([P, CHUNK], U8, align_bytes=64)
+            nc.vector.quantize_mx(out=cc[:].bitcast(FP8X4), scales=cs[:], in_=state["g%d" % j][:])
+            state["c%d" % j] = (cc, cs)
+
+        def relu_tiles(q, on_scalar):
+            c = q // 2
+            tiles = (0, 1) if q % 2 == 0 else (2, 3)
+            return [a - tiles[0] for a in tiles if (c >= RELU_S_FROM or a >= 4 - RELU_S_TILES) == on_scalar]
+
+        def stage2(q):
+            if q < 0 or q >= N_UNITS:
+                return
+            c = q // 2
+            ob = ob_pool.tile([P, 2 * E], F32)
+            state["o%d" % q] = ob
+            b1_bc = state["b1_bc"]
+            banks = []
+            for i in range(2):
+                a = 2 * (q % 2) + i
+                acc2 = ps_s2.tile([P, E], F32, tag="ps")
+                for g in range(2):
+                    cc, cs = state["c%d" % (2 * c + g)]
+                    mc, ms = state["m%d" % g]
+                    nc.tensor.matmul_mx(
+                        out=acc2[:],
+                        lhsT=cc[:, a * P : (a + 1) * P].bitcast(FP8X4),
+                        lhsT_scale=cs[:, a * P : (a + 1) * P],
+                        rhs=mc[:].bitcast(FP8X4),
+                        rhs_scale=ms[:],
+                        start=(g == 0),
+                        stop=(g == 1),
+                    )
+                banks.append(acc2)
+            for i in range(2):
+                nc.vector.tensor_tensor(
+                    out=ob[:, i * E : (i + 1) * E], in0=banks[i][:], in1=b1_bc[:], op=ALU.add
+                )
+
+        def relu_vector(q):
+            if q < 0 or q >= N_UNITS:
+                return
+            mine = relu_tiles(q, False)
+            if mine:
+                span = state["o%d" % q][:, mine[0] * E : (mine[-1] + 1) * E]
+                nc.vector.tensor_scalar_max(out=span, in0=span, scalar1=0.0)
+
+        def relu_scalar_and_store(q):
+            if q < 0 or q >= N_UNITS:
+                return
+            c = q // 2
+            ob = state["o%d" % q]
+            rows = of[c * CHUNK : (c + 1) * CHUNK, :].rearrange("(p a) f -> p a f", a=4)
+            first = 2 * (q % 2)
+            mine = relu_tiles(q, True)
+            for i in mine:
+                span = ob[:, i * E : (i + 1) * E]
+                nc.scalar.activation(out=span, in_=span, func=ACT.Relu)
+                if len(mine) == 2:
+                    nc.sync.dma_start(out=rows[:, first + i, :], in_=span)
+            if len(mine) < 2:
+                nc.sync.dma_start(
+                    out=rows[:, first : first + 2, :], in_=ob[:].rearrange("p (a f) -> p a f", a=2)
+                )
+
+        prepare_biases()
+        state["w0"] = weight_unit(hw_raw[:].bitcast(F32), 256, 0, "hw", True)
+        tq(0)
+        state["w1"] = weight_unit(vw_raw[:].bitcast(F32), 256, 0, "vw", True)
+        tq(1)
+        for m in range(N_UNITS + S2_LAG + 1):
+            stage1(m)
+            regroup(m)
+            if m == 0:
+                state["m0"] = weight_unit(w1_raw[:].bitcast(F32), 512, 0, "w1a", False)
+            if m == 1:
+                state["m1"] = weight_unit(w1_raw[:].bitcast(F32), 512, 256, "w1b", False)
+            tq(m + 2)
+            quantise2(m)
+            relu_scalar_and_store(m - S2_LAG - 1)
+            stage2(m - S2_LAG)
+            relu_vector(m - S2_LAG)

@@ -18,12 +18,8 @@ N_CHUNKS = 8
 N_UNITS = 2 * N_CHUNKS
 FLOPS = 2 * 4096 * 512 * 512 * 2 + 2 * 4096 * 1024 * 512
 
-PINNED = False
-XT_V_BELOW = 2
-X1_V_BELOW = 2
-RELU_S_FROM = 6
-RELU_S_TILES = 2
-S2_LAG = 2
+S2_LAG = 3
+DEFERRED_FROM = 10
 
 
 def tile_bispa_pa_t_kernel(
@@ -34,136 +30,122 @@ def tile_bispa_pa_t_kernel(
         consts = ctx.enter_context(tc.tile_pool(name="consts", bufs=1))
         raw = ctx.enter_context(tc.tile_pool(name="raw", bufs=1))
         wq = ctx.enter_context(tc.tile_pool(name="wq", bufs=1))
-        grp_pool = ctx.enter_context(tc.tile_pool(name="grp", bufs=3))
+        grp_pool = ctx.enter_context(tc.tile_pool(name="grp", bufs=4))
         xq = ctx.enter_context(tc.tile_pool(name="xq", bufs=4))
         pl_pool = ctx.enter_context(tc.tile_pool(name="pl", bufs=3))
         g2_pool = ctx.enter_context(tc.tile_pool(name="g2", bufs=3))
         cq = ctx.enter_context(tc.tile_pool(name="cq", bufs=6))
-        ob_pool = ctx.enter_context(tc.tile_pool(name="ob", bufs=4))
-        ps_tp = ctx.enter_context(tc.psum_pool(name="ps", bufs=8))
-        ps_s1 = ps_tp
-        ps_s2 = ps_tp
-        if PINNED:
-            ctx.enter_context(tc.manual_schedule())
+        ob_pool = ctx.enter_context(tc.tile_pool(name="ob", bufs=8))
+        psum = ctx.enter_context(tc.psum_pool(name="ps", bufs=8))
+        ctx.enter_context(tc.manual_schedule())
 
         hx = h_ctx.flatten_outer_dims()
         vx = v_ctx.flatten_outer_dims()
         of = out.flatten_outer_dims()
 
+        ident = consts.tile([P, P], F32, name="ident")
+        make_identity(nc, ident[:])
         zb = consts.tile([P, E], BF16, name="zb")
         nc.vector.memset(zb[:], 0.0)
         zrow = consts.tile([P, E], BF16, name="zrow")
         nc.vector.memset(zrow[:], 0.0)
         ones = consts.tile([P, P], BF16, name="ones")
         nc.vector.memset(ones[:], 1.0)
-        ident = consts.tile([P, P], F32, name="ident")
-        make_identity(nc, ident[:])
-        nc.sync.dma_start(out=zb[0:1, :], in_=h_out_b.rearrange("(o n) -> o n", o=1))
-        nc.sync.dma_start(out=zb[1:2, :], in_=v_out_b.rearrange("(o n) -> o n", o=1))
-        nc.sync.dma_start(out=zrow[0:1, :], in_=mlp_b1.rearrange("(o n) -> o n", o=1))
+
+        raw_tiles = {}
 
         def load_proj(w, name):
             t = raw.tile([P, 4 * E], BF16, name=name)
-            nc.sync.dma_start(
-                out=t[:].rearrange("q (t k) -> q t k", t=4),
-                in_=w.rearrange("(q t) k -> q t k", t=4),
-            )
-            return t
+            nc.sync.dma_start(out=t[:].rearrange("q (t k) -> q t k", t=4), in_=w.rearrange("(q t) k -> q t k", t=4))
+            raw_tiles[name] = (t[:].bitcast(F32), 256, 0)
 
-        def load_ctx(x, c, name):
+        def load_ctx(j):
+            x = vx if j % 2 else hx
+            c = j // 2
+            name = "x%d" % j
             t = raw.tile([P, 4 * E], BF16, name=name)
             nc.sync.dma_start(
                 out=t[:].rearrange("p (a k) -> p a k", a=4),
                 in_=x[c * CHUNK : (c + 1) * CHUNK, :].rearrange("(p a) k -> p a k", a=4),
             )
-            return t
+            raw_tiles[name] = (t[:].bitcast(F32), 256, 0)
 
-        ctx_raw = {}
-        hw_raw = load_proj(h_out_w, "hw_raw")
-        ctx_raw[0] = load_ctx(hx, 0, "x0")
-        vw_raw = load_proj(v_out_w, "vw_raw")
-        ctx_raw[1] = load_ctx(vx, 0, "x1")
+        load_proj(h_out_w, "hw")
+        load_ctx(0)
+        nc.sync.dma_start(out=zb[0:1, :], in_=h_out_b.rearrange("(o n) -> o n", o=1))
+        nc.sync.dma_start(out=zb[1:2, :], in_=v_out_b.rearrange("(o n) -> o n", o=1))
+        nc.sync.dma_start(out=zrow[0:1, :], in_=mlp_b1.rearrange("(o n) -> o n", o=1))
+        load_proj(v_out_w, "vw")
+        load_ctx(1)
         w1_raw = raw.tile([P, 4 * 2 * E], BF16, name="w1_raw")
-        nc.sync.dma_start(
-            out=w1_raw[:].rearrange("p (j k) -> p j k", j=4),
-            in_=mlp_w1.rearrange("(j p) k -> p j k", p=P),
-        )
-        for c in range(1, N_CHUNKS):
-            ctx_raw[2 * c] = load_ctx(hx, c, "x%d" % (2 * c))
-            ctx_raw[2 * c + 1] = load_ctx(vx, c, "x%d" % (2 * c + 1))
+        nc.sync.dma_start(out=w1_raw[:].rearrange("p (j k) -> p j k", j=4), in_=mlp_w1.rearrange("(j p) k -> p j k", p=P))
+        raw_tiles["w1a"] = (w1_raw[:].bitcast(F32), 512, 0)
+        raw_tiles["w1b"] = (w1_raw[:].bitcast(F32), 512, 256)
+        for j in range(2, N_UNITS):
+            load_ctx(j)
 
-        def copy_out(on_vector, dst, src):
+        st = {}
+
+        def bank():
+            b = psum.tile([P, E], F32, tag="ps", name="bank")
+            return b
+
+        def transpose(n, half):
+            words, row_words, first = raw_tiles[n]
+            b = bank()
+            for jj in range(2):
+                for u in range(2):
+                    start = (2 * half + jj) * row_words + first + u
+                    nc.tensor.transpose(
+                        b[:, u * 256 + jj * P : u * 256 + (jj + 1) * P], words[:, start : start + 2 * P - 1 : 2], ident[:]
+                    )
+            st["T", n, half] = b
+
+        def exit_t(n, half, on_vector=False):
+            if half == 0:
+                grp = grp_pool.tile([P, 4 * E], BF16, align_bytes=64, name="grp")
+                st["grp", n] = grp
+            dst = st["grp", n][:].bitcast(F32)[:, half * E : (half + 1) * E].rearrange("p (r u) -> p r u", u=2)
+            src = st["T", n, half][:].rearrange("p (u r) -> p r u", u=2)
             if on_vector:
                 nc.vector.tensor_copy(out=dst, in_=src)
             else:
                 nc.scalar.copy(out=dst, in_=src)
 
-        def transpose_quantise(words, row_words, first_word, codes, scales, second_on_vector):
-            grp = grp_pool.tile([P, 4 * E], BF16, align_bytes=64)
-            grp_words = grp[:].bitcast(F32)
-            for half in range(2):
-                bank = ps_tp.tile([P, E], F32, tag="ps")
-                for jj in range(2):
-                    for u in range(2):
-                        start = (2 * half + jj) * row_words + first_word + u
-                        nc.tensor.transpose(
-                            bank[:, u * 256 + jj * P : u * 256 + (jj + 1) * P],
-                            words[:, start : start + 2 * P - 1 : 2],
-                            ident[:],
-                        )
-                copy_out(
-                    second_on_vector and half == 1,
-                    grp_words[:, half * E : (half + 1) * E].rearrange("p (r u) -> p r u", u=2),
-                    bank[:].rearrange("p (u r) -> p r u", u=2),
-                )
-            nc.vector.quantize_mx(out=codes[:].bitcast(FP8X4), scales=scales[:], in_=grp[:])
+        def quantise(n):
+            if n[0] == "x":
+                codes = xq.tile([P, E], U32, align_bytes=64, name="xc")
+                scales = xq.tile([P, E], U8, align_bytes=64, name="xs")
+            else:
+                codes = wq.tile([P, E], U32, name=n + "_c", align_bytes=64)
+                scales = wq.tile([P, E], U8, name=n + "_s", align_bytes=64)
+            nc.vector.quantize_mx(out=codes[:].bitcast(FP8X4), scales=scales[:], in_=st["grp", n][:])
+            st["q", n] = (codes, scales)
 
-        def weight_unit(words, row_words, first_word, name, second_on_vector):
-            codes = wq.tile([P, E], U32, name=name + "_c", align_bytes=64)
-            scales = wq.tile([P, E], U8, name=name + "_s", align_bytes=64)
-            transpose_quantise(words, row_words, first_word, codes, scales, second_on_vector)
-            return codes, scales
-
-        state = {}
-
-        def prepare_biases():
-            bank = ps_tp.tile([P, E], F32, tag="ps")
+        def biases():
+            b = bank()
             zw = zb[:].bitcast(F32)
             for u in range(2):
-                nc.tensor.transpose(bank[:, u * P : (u + 1) * P], zw[:, u : u + 2 * P - 1 : 2], ident[:])
+                nc.tensor.transpose(b[:, u * P : (u + 1) * P], zw[:, u : u + 2 * P - 1 : 2], ident[:])
             bias8 = consts.tile([P, 8], F32, name="bias8")
             nc.vector.tensor_copy(
                 out=bias8[:].rearrange("p (s u e) -> p u s e", s=2, u=2),
-                in_=bank[:].bitcast(BF16)[:, 0 : 4 * P].rearrange("p (u x) -> p u x", u=2)[:, :, 0:4].rearrange("p u (s e) -> p u s e", s=2),
+                in_=b[:].bitcast(BF16)[:, 0 : 4 * P].rearrange("p (u x) -> p u x", u=2)[:, :, 0:4].rearrange("p u (s e) -> p u s e", s=2),
             )
-            state["bias8"] = bias8
-            acc = ps_s2.tile([P, E], F32, tag="ps")
+            st["bias8"] = bias8
+            acc = bank()
             nc.tensor.matmul(out=acc[:], lhsT=ones[:], rhs=zrow[:], start=True, stop=True)
             b1_bc = consts.tile([P, E], F32, name="b1_bc")
             nc.vector.tensor_copy(out=b1_bc[:], in_=acc[:])
-            state["b1_bc"] = b1_bc
-
-        def tq(j):
-            if j < 0 or j >= N_UNITS:
-                return
-            xc = xq.tile([P, E], U32, align_bytes=64)
-            xs = xq.tile([P, E], U8, align_bytes=64)
-            transpose_quantise(ctx_raw[j][:].bitcast(F32), 256, 0, xc, xs, j < XT_V_BELOW)
-            state["x%d" % j] = (xc, xs)
+            st["b1"] = b1_bc
 
         def stage1(j):
-            if j < 0 or j >= N_UNITS:
-                return
-            s = j % 2
-            wc, ws = state["w%d" % s]
-            xc, xs = state["x%d" % j]
-            bias8 = state["bias8"]
-            planar = pl_pool.tile([P, 4 * CHUNK], BF16)
-            banks = []
+            wc, ws = st["q", "hw" if j % 2 == 0 else "vw"]
+            xc, xs = st["q", "x%d" % j]
             for t in range(4):
-                acc1 = ps_s1.tile([P, CHUNK], F32, tag="ps")
+                b = bank()
                 nc.tensor.matmul_mx(
-                    out=acc1[:],
+                    out=b[:],
                     lhsT=wc[:, t * P : (t + 1) * P].bitcast(FP8X4),
                     lhsT_scale=ws[:, t * P : (t + 1) * P],
                     rhs=xc[:].bitcast(FP8X4),
@@ -171,109 +153,144 @@ def tile_bispa_pa_t_kernel(
                     start=True,
                     stop=True,
                 )
-                banks.append(acc1)
-            for t in range(4):
-                dst = planar[:, t * CHUNK : (t + 1) * CHUNK]
-                b = bias8[:, 4 * s + t : 4 * s + t + 1]
-                if j < X1_V_BELOW and t % 2 == 1:
-                    nc.vector.tensor_scalar_add(out=dst, in0=banks[t][:], scalar1=b)
-                else:
-                    nc.scalar.activation(out=dst, in_=banks[t][:], func=ACT.Identity, bias=b, scale=1.0)
-            state["p%d" % j] = planar
+                st["M", j, t] = b
+
+        def exit_1(j, t, on_vector=False):
+            if t == 0:
+                planar = pl_pool.tile([P, 4 * CHUNK], BF16, name="planar")
+                st["planar", j] = planar
+            dst = st["planar", j][:, t * CHUNK : (t + 1) * CHUNK]
+            i = 4 * (j % 2) + t
+            b = st["bias8"][:, i : i + 1]
+            if on_vector:
+                nc.vector.tensor_scalar_add(out=dst, in0=st["M", j, t][:], scalar1=b)
+            else:
+                nc.scalar.activation(out=dst, in_=st["M", j, t][:], func=ACT.Identity, bias=b, scale=1.0)
 
         def regroup(j):
-            if j < 0 or j >= N_UNITS:
-                return
-            planar = state["p%d" % j]
-            g2 = g2_pool.tile([P, 4 * CHUNK], BF16, align_bytes=64)
+            g2 = g2_pool.tile([P, 4 * CHUNK], BF16, align_bytes=64, name="g2")
             nc.vector.tensor_copy(
                 out=g2[:].rearrange("p (c i t) -> p c t i", i=4, t=4),
-                in_=planar[:].rearrange("p (t c i) -> p c t i", t=4, i=4),
+                in_=st["planar", j][:].rearrange("p (t c i) -> p c t i", t=4, i=4),
             )
-            state["g%d" % j] = g2
+            st["g2", j] = g2
 
         def quantise2(j):
-            if j < 0 or j >= N_UNITS:
-                return
-            cc = cq.tile([P, CHUNK], U32, align_bytes=64)
-            cs = cq.tile([P, CHUNK], U8, align_bytes=64)
-            nc.vector.quantize_mx(out=cc[:].bitcast(FP8X4), scales=cs[:], in_=state["g%d" % j][:])
-            state["c%d" % j] = (cc, cs)
+            cc = cq.tile([P, CHUNK], U32, align_bytes=64, name="cc")
+            cs = cq.tile([P, CHUNK], U8, align_bytes=64, name="cs")
+            nc.vector.quantize_mx(out=cc[:].bitcast(FP8X4), scales=cs[:], in_=st["g2", j][:])
+            st["c", j] = (cc, cs)
 
-        def relu_tiles(q, on_scalar):
-            c = q // 2
-            tiles = (0, 1) if q % 2 == 0 else (2, 3)
-            return [a - tiles[0] for a in tiles if (c >= RELU_S_FROM or a >= 4 - RELU_S_TILES) == on_scalar]
-
-        def stage2(q):
-            if q < 0 or q >= N_UNITS:
-                return
-            c = q // 2
-            ob = ob_pool.tile([P, 2 * E], F32)
-            state["o%d" % q] = ob
-            b1_bc = state["b1_bc"]
-            banks = []
-            for i in range(2):
-                a = 2 * (q % 2) + i
-                acc2 = ps_s2.tile([P, E], F32, tag="ps")
-                for g in range(2):
-                    cc, cs = state["c%d" % (2 * c + g)]
-                    mc, ms = state["m%d" % g]
-                    nc.tensor.matmul_mx(
-                        out=acc2[:],
-                        lhsT=cc[:, a * P : (a + 1) * P].bitcast(FP8X4),
-                        lhsT_scale=cs[:, a * P : (a + 1) * P],
-                        rhs=mc[:].bitcast(FP8X4),
-                        rhs_scale=ms[:],
-                        start=(g == 0),
-                        stop=(g == 1),
-                    )
-                banks.append(acc2)
-            for i in range(2):
-                nc.vector.tensor_tensor(
-                    out=ob[:, i * E : (i + 1) * E], in0=banks[i][:], in1=b1_bc[:], op=ALU.add
+        def stage2(p, i):
+            c = p // 2
+            a = 2 * (p % 2) + i
+            b = bank()
+            for g in range(2):
+                cc, cs = st["c", 2 * c + g]
+                mc, ms = st["q", "w1a" if g == 0 else "w1b"]
+                nc.tensor.matmul_mx(
+                    out=b[:],
+                    lhsT=cc[:, a * P : (a + 1) * P].bitcast(FP8X4),
+                    lhsT_scale=cs[:, a * P : (a + 1) * P],
+                    rhs=mc[:].bitcast(FP8X4),
+                    rhs_scale=ms[:],
+                    start=(g == 0),
+                    stop=(g == 1),
                 )
+            st["N", p, i] = b
 
-        def relu_vector(q):
-            if q < 0 or q >= N_UNITS:
-                return
-            mine = relu_tiles(q, False)
-            if mine:
-                span = state["o%d" % q][:, mine[0] * E : (mine[-1] + 1) * E]
+        def add_b1(p, i):
+            if i == 0:
+                ob = ob_pool.tile([P, 2 * E], F32, name="ob")
+                st["ob", p] = ob
+            nc.vector.tensor_tensor(
+                out=st["ob", p][:, i * E : (i + 1) * E], in0=st["N", p, i][:], in1=st["b1"][:], op=ALU.add
+            )
+
+        def relu(p, i, scalar):
+            span = st["ob", p][:, i * E : (i + 1) * E]
+            if scalar:
+                nc.scalar.activation(out=span, in_=span, func=ACT.Relu)
+            else:
                 nc.vector.tensor_scalar_max(out=span, in0=span, scalar1=0.0)
 
-        def relu_scalar_and_store(q):
-            if q < 0 or q >= N_UNITS:
-                return
-            c = q // 2
-            ob = state["o%d" % q]
-            rows = of[c * CHUNK : (c + 1) * CHUNK, :].rearrange("(p a) f -> p a f", a=4)
-            first = 2 * (q % 2)
-            mine = relu_tiles(q, True)
-            for i in mine:
-                span = ob[:, i * E : (i + 1) * E]
-                nc.scalar.activation(out=span, in_=span, func=ACT.Relu)
-                if len(mine) == 2:
-                    nc.sync.dma_start(out=rows[:, first + i, :], in_=span)
-            if len(mine) < 2:
-                nc.sync.dma_start(
-                    out=rows[:, first : first + 2, :], in_=ob[:].rearrange("p (a f) -> p a f", a=2)
-                )
+        def relu_step(p):
+            if p < DEFERRED_FROM:
+                return p + S2_LAG + 2
+            return max(N_UNITS - 1, p + S2_LAG + 1)
 
-        prepare_biases()
-        state["w0"] = weight_unit(hw_raw[:].bitcast(F32), 256, 0, "hw", True)
-        tq(0)
-        state["w1"] = weight_unit(vw_raw[:].bitcast(F32), 256, 0, "vw", True)
-        tq(1)
-        for m in range(N_UNITS + S2_LAG + 1):
-            stage1(m)
-            regroup(m)
+        def store(p, tiles):
+            c = p // 2
+            rows = of[c * CHUNK : (c + 1) * CHUNK, :].rearrange("(p a) f -> p a f", a=4)
+            first = 2 * (p % 2)
+            lo, hi = tiles[0], tiles[-1] + 1
+            nc.sync.dma_start(
+                out=rows[:, first + lo : first + hi, :],
+                in_=st["ob", p][:, lo * E : hi * E].rearrange("p (a f) -> p a f", a=hi - lo),
+            )
+
+        def unit(m):
+            return 0 <= m < N_UNITS
+
+        for n in ("hw", "x0"):
+            transpose(n, 0)
+            transpose(n, 1)
+        exit_t("hw", 0)
+        exit_t("hw", 1, True)
+        quantise("hw")
+        exit_t("x0", 0)
+        exit_t("x0", 1)
+        biases()
+        quantise("x0")
+        for n in ("vw", "x1"):
+            transpose(n, 0)
+            transpose(n, 1)
+            exit_t(n, 0)
+            exit_t(n, 1)
+            quantise(n)
+
+        for m in range(N_UNITS + 5):
+            x = "x%d" % (m + 2)
+            p = m - S2_LAG
+            if unit(m):
+                stage1(m)
+            if unit(p):
+                stage2(p, 0)
+                stage2(p, 1)
+            if unit(m):
+                for t in range(4):
+                    exit_1(m, t, m == 1 and t == 3)
             if m == 0:
-                state["m0"] = weight_unit(w1_raw[:].bitcast(F32), 512, 0, "w1a", False)
-            if m == 1:
-                state["m1"] = weight_unit(w1_raw[:].bitcast(F32), 512, 256, "w1b", False)
-            tq(m + 2)
-            quantise2(m)
-            relu_scalar_and_store(m - S2_LAG - 1)
-            stage2(m - S2_LAG)
-            relu_vector(m - S2_LAG)
+                for n in ("w1a", "w1b"):
+                    for half in range(2):
+                        transpose(n, half)
+                        exit_t(n, half, n == "w1a")
+            if unit(m + 2):
+                for half in range(2):
+                    transpose(x, half)
+                    exit_t(x, half, m == 1 and half == 1)
+            for q in range(N_UNITS):
+                if relu_step(q) == m:
+                    if q >= DEFERRED_FROM and q < N_UNITS - 2:
+                        relu(q, 0, True)
+                        store(q, (0,))
+                    relu(q, 1, True)
+                    if q >= DEFERRED_FROM:
+                        store(q, (1,))
+            if unit(p):
+                add_b1(p, 0)
+                add_b1(p, 1)
+            for q in range(N_UNITS):
+                if relu_step(q) == m:
+                    if q < DEFERRED_FROM or q >= N_UNITS - 2:
+                        relu(q, 0, False)
+                        store(q, (0, 1) if q < DEFERRED_FROM else (0,))
+            if unit(m):
+                regroup(m)
+            if m == 0:
+                quantise("w1a")
+                quantise("w1b")
+            if unit(m + 2):
+                quantise(x)
+            if unit(m):
+                quantise2(m)

@@ -56,7 +56,11 @@ def tile_bispa_pa_t_kernel(
 
         def load_proj(w, name):
             t = raw.tile([P, 4 * E], BF16, name=name)
-            nc.sync.dma_start(out=t[:].rearrange("q (t k) -> q t k", t=4), in_=w.rearrange("(q t) k -> q t k", t=4))
+            for h in range(2):
+                nc.sync.dma_start(
+                    out=t[:].rearrange("q (t k) -> q t k", t=4)[:, 2 * h : 2 * h + 2, :],
+                    in_=w.rearrange("(q t) k -> q t k", t=4)[:, 2 * h : 2 * h + 2, :],
+                )
             raw_tiles[name] = (t[:].bitcast(F32), 256, 0)
 
         def load_ctx(j):
@@ -64,10 +68,12 @@ def tile_bispa_pa_t_kernel(
             c = j // 2
             name = "x%d" % j
             t = raw.tile([P, 4 * E], BF16, name=name)
-            nc.sync.dma_start(
-                out=t[:].rearrange("p (a k) -> p a k", a=4),
-                in_=x[c * CHUNK : (c + 1) * CHUNK, :].rearrange("(p a) k -> p a k", a=4),
-            )
+            step = 2 if j < 2 else 4
+            for a in range(0, 4, step):
+                nc.sync.dma_start(
+                    out=t[:].rearrange("p (a k) -> p a k", a=4)[:, a : a + step, :],
+                    in_=x[c * CHUNK : (c + 1) * CHUNK, :].rearrange("(p a) k -> p a k", a=4)[:, a : a + step, :],
+                )
             raw_tiles[name] = (t[:].bitcast(F32), 256, 0)
 
         load_proj(h_out_w, "hw")
@@ -214,7 +220,7 @@ def tile_bispa_pa_t_kernel(
             else:
                 nc.vector.tensor_scalar_max(out=span, in0=span, scalar1=0.0)
 
-        def relu_step(p):
+        def scalar_relu_step(p):
             if p < DEFERRED_FROM:
                 return p + S2_LAG + 2
             return max(N_UNITS - 1, p + S2_LAG + 1)
@@ -246,7 +252,7 @@ def tile_bispa_pa_t_kernel(
             transpose(n, 0)
             transpose(n, 1)
             exit_t(n, 0)
-            exit_t(n, 1)
+            exit_t(n, 1, n == "vw")
             quantise(n)
 
         for m in range(N_UNITS + 5):
@@ -254,10 +260,6 @@ def tile_bispa_pa_t_kernel(
             p = m - S2_LAG
             if unit(m):
                 stage1(m)
-            if unit(p):
-                stage2(p, 0)
-                stage2(p, 1)
-            if unit(m):
                 for t in range(4):
                     exit_1(m, t, m == 1 and t == 3)
             if m == 0:
@@ -269,28 +271,28 @@ def tile_bispa_pa_t_kernel(
                 for half in range(2):
                     transpose(x, half)
                     exit_t(x, half, m == 1 and half == 1)
+            if unit(p):
+                stage2(p, 0)
+                stage2(p, 1)
             for q in range(N_UNITS):
-                if relu_step(q) == m:
-                    if q >= DEFERRED_FROM and q < N_UNITS - 2:
+                if scalar_relu_step(q) == m:
+                    if q >= DEFERRED_FROM:
                         relu(q, 0, True)
                         store(q, (0,))
                     relu(q, 1, True)
-                    if q >= DEFERRED_FROM:
-                        store(q, (1,))
+                    store(q, (1,) if q >= DEFERRED_FROM else (0, 1))
             if unit(p):
                 add_b1(p, 0)
-                add_b1(p, 1)
-            for q in range(N_UNITS):
-                if relu_step(q) == m:
-                    if q < DEFERRED_FROM or q >= N_UNITS - 2:
-                        relu(q, 0, False)
-                        store(q, (0, 1) if q < DEFERRED_FROM else (0,))
             if unit(m):
                 regroup(m)
+            if unit(p):
+                add_b1(p, 1)
             if m == 0:
                 quantise("w1a")
                 quantise("w1b")
             if unit(m + 2):
                 quantise(x)
+            if unit(p - 1) and p - 1 < DEFERRED_FROM:
+                relu(p - 1, 0, False)
             if unit(m):
                 quantise2(m)

@@ -238,6 +238,9 @@ def tile_bispa_pa_t_kernel(
         def unit(m):
             return 0 <= m < N_UNITS
 
+        def pair_on_vector(p):
+            return p in (1, 5)
+
         for n in ("hw", "x0"):
             transpose(n, 0)
             transpose(n, 1)
@@ -275,7 +278,7 @@ def tile_bispa_pa_t_kernel(
                 stage2(p, 0)
                 stage2(p, 1)
             for q in range(N_UNITS):
-                if scalar_relu_step(q) == m:
+                if scalar_relu_step(q) == m and not pair_on_vector(q):
                     if q >= DEFERRED_FROM:
                         relu(q, 0, True)
                         store(q, (0,))
@@ -292,7 +295,11 @@ def tile_bispa_pa_t_kernel(
                 quantise("w1b")
             if unit(m + 2):
                 quantise(x)
-            if unit(p - 1) and p - 1 < DEFERRED_FROM:
+            if unit(p - 1) and pair_on_vector(p - 1):
+                span = st["ob", p - 1][:]
+                nc.vector.tensor_scalar_max(out=span, in0=span, scalar1=0.0)
+                store(p - 1, (0, 1))
+            elif unit(p - 1) and p - 1 < DEFERRED_FROM:
                 relu(p - 1, 0, False)
             if unit(m):
                 quantise2(m)

@@ -176,8 +176,8 @@ def tile_bispa_pa_t_kernel(
         def regroup(j):
             g2 = g2_pool.tile([P, 4 * CHUNK], BF16, align_bytes=64, name="g2")
             nc.vector.tensor_copy(
-                out=g2[:].rearrange("p (c i t) -> p c t i", i=4, t=4),
-                in_=st["planar", j][:].rearrange("p (t c i) -> p c t i", t=4, i=4),
+                out=g2[:].rearrange("p (c h i t) -> p h c t i", h=2, i=4, t=4),
+                in_=st["planar", j][:].rearrange("p (t c h i) -> p h c t i", t=4, h=2, i=4),
             )
             st["g2", j] = g2
 

@@ -56,10 +56,11 @@ def tile_bispa_pa_t_kernel(
 
         def load_proj(w, name):
             t = raw.tile([P, 4 * E], BF16, name=name)
-            for h in range(2):
+            step = 2 if name == "hw" else 4
+            for a in range(0, 4, step):
                 nc.sync.dma_start(
-                    out=t[:].rearrange("q (t k) -> q t k", t=4)[:, 2 * h : 2 * h + 2, :],
-                    in_=w.rearrange("(q t) k -> q t k", t=4)[:, 2 * h : 2 * h + 2, :],
+                    out=t[:].rearrange("q (t k) -> q t k", t=4)[:, a : a + step, :],
+                    in_=w.rearrange("(q t) k -> q t k", t=4)[:, a : a + step, :],
                 )
             raw_tiles[name] = (t[:].bitcast(F32), 256, 0)
 
@@ -68,7 +69,7 @@ def tile_bispa_pa_t_kernel(
             c = j // 2
             name = "x%d" % j
             t = raw.tile([P, 4 * E], BF16, name=name)
-            step = 2 if j < 2 else 4
+            step = 2 if j == 0 else 4
             for a in range(0, 4, step):
                 nc.sync.dma_start(
                     out=t[:].rearrange("p (a k) -> p a k", a=4)[:, a : a + step, :],
@@ -76,11 +77,11 @@ def tile_bispa_pa_t_kernel(
                 )
             raw_tiles[name] = (t[:].bitcast(F32), 256, 0)
 
+        nc.scalar.dma_start(out=zb[0:1, :], in_=h_out_b.rearrange("(o n) -> o n", o=1))
+        nc.scalar.dma_start(out=zb[1:2, :], in_=v_out_b.rearrange("(o n) -> o n", o=1))
+        nc.scalar.dma_start(out=zrow[0:1, :], in_=mlp_b1.rearrange("(o n) -> o n", o=1))
         load_proj(h_out_w, "hw")
         load_ctx(0)
-        nc.sync.dma_start(out=zb[0:1, :], in_=h_out_b.rearrange("(o n) -> o n", o=1))
-        nc.sync.dma_start(out=zb[1:2, :], in_=v_out_b.rearrange("(o n) -> o n", o=1))
-        nc.sync.dma_start(out=zrow[0:1, :], in_=mlp_b1.rearrange("(o n) -> o n", o=1))
         load_proj(v_out_w, "vw")
         load_ctx(1)
         w1_raw = raw.tile([P, 4 * 2 * E], BF16, name="w1_raw")
@@ -239,7 +240,7 @@ def tile_bispa_pa_t_kernel(
             return 0 <= m < N_UNITS
 
         def pair_on_vector(p):
-            return p in (1, 5)
+            return p % 3 != 0 and p < DEFERRED_FROM
 
         for n in ("hw", "x0"):
             transpose(n, 0)
@@ -279,11 +280,14 @@ def tile_bispa_pa_t_kernel(
                 stage2(p, 1)
             for q in range(N_UNITS):
                 if scalar_relu_step(q) == m and not pair_on_vector(q):
-                    if q >= DEFERRED_FROM:
-                        relu(q, 0, True)
-                        store(q, (0,))
-                    relu(q, 1, True)
-                    store(q, (1,) if q >= DEFERRED_FROM else (0, 1))
+                    if q < DEFERRED_FROM:
+                        span = st["ob", q][:]
+                        nc.scalar.activation(out=span, in_=span, func=ACT.Relu)
+                        store(q, (0, 1))
+                    else:
+                        for i in range(2):
+                            relu(q, i, True)
+                            store(q, (i,))
             if unit(p):
                 add_b1(p, 0)
             if unit(m):
@@ -299,7 +303,5 @@ def tile_bispa_pa_t_kernel(
                 span = st["ob", p - 1][:]
                 nc.vector.tensor_scalar_max(out=span, in0=span, scalar1=0.0)
                 store(p - 1, (0, 1))
-            elif unit(p - 1) and p - 1 < DEFERRED_FROM:
-                relu(p - 1, 0, False)
             if unit(m):
                 quantise2(m)

from contextlib import ExitStack

import concourse.mybir as mybir
from concourse.masks import make_identity

F32 = mybir.dt.float32
BF16 = mybir.dt.bfloat16
U32 = mybir.dt.uint32
U8 = mybir.dt.uint8
FP8X4 = mybir.dt.float8_e4m3fn_x4
ACT = mybir.ActivationFunctionType
ALU = mybir.AluOpType

P = 128
E = 512
CHUNK = 512
N_CHUNKS = 8
N_UNITS = 2 * N_CHUNKS
FLOPS = 2 * 4096 * 512 * 512 * 2 + 2 * 4096 * 1024 * 512

S2_LAG = 3
DEFERRED_FROM = 10


def tile_bispa_pa_t_kernel(
    tc, h_ctx, v_ctx, h_out_w, h_out_b, v_out_w, v_out_b, mlp_w1, mlp_b1, out
):
    nc = tc.nc
    with ExitStack() as ctx:
        consts = ctx.enter_context(tc.tile_pool(name="consts", bufs=1))
        raw = ctx.enter_context(tc.tile_pool(name="raw", bufs=1))
        wq = ctx.enter_context(tc.tile_pool(name="wq", bufs=1))
        grp_pool = ctx.enter_context(tc.tile_pool(name="grp", bufs=4))
        xq = ctx.enter_context(tc.tile_pool(name="xq", bufs=4))
        pl_pool = ctx.enter_context(tc.tile_pool(name="pl", bufs=3))
        g2_pool = ctx.enter_context(tc.tile_pool(name="g2", bufs=3))
        cq = ctx.enter_context(tc.tile_pool(name="cq", bufs=6))
        ob_pool = ctx.enter_context(tc.tile_pool(name="ob", bufs=8))
        psum = ctx.enter_context(tc.psum_pool(name="ps", bufs=8))
        ctx.enter_context(tc.manual_schedule())

        hx = h_ctx.flatten_outer_dims()
        vx = v_ctx.flatten_outer_dims()
        of = out.flatten_outer_dims()

        ident = consts.tile([P, P], F32, name="ident")
        make_identity(nc, ident[:])
        zb = consts.tile([P, E], BF16, name="zb")
        nc.vector.memset(zb[:], 0.0)
        zrow = consts.tile([P, E], BF16, name="zrow")
        nc.vector.memset(zrow[:], 0.0)
        ones = consts.tile([P, P], BF16, name="ones")
        nc.vector.memset(ones[:], 1.0)

        raw_tiles = {}

        def load_proj(w, name):
            t = raw.tile([P, 4 * E], BF16, name=name)
            step = 2 if name == "hw" else 4
            for a in range(0, 4, step):
                nc.sync.dma_start(
                    out=t[:].rearrange("q (t k) -> q t k", t=4)[:, a : a + step, :],
                    in_=w.rearrange("(q t) k -> q t k", t=4)[:, a : a + step, :],
                )
            raw_tiles[name] = (t[:].bitcast(F32), 256, 0)

        def load_ctx(j):
            x = vx if j % 2 else hx
            c = j // 2
            name = "x%d" % j
            t = raw.tile([P, 4 * E], BF16, name=name)
            step = 2 if j == 0 else 4
            for a in range(0, 4, step):
                nc.sync.dma_start(
                    out=t[:].rearrange("p (a k) -> p a k", a=4)[:, a : a + step, :],
                    in_=x[c * CHUNK : (c + 1) * CHUNK, :].rearrange("(p a) k -> p a k", a=4)[:, a : a + step, :],
                )
            raw_tiles[name] = (t[:].bitcast(F32), 256, 0)

        nc.scalar.dma_start(out=zb[0:1, :], in_=h_out_b.rearrange("(o n) -> o n", o=1))
        nc.scalar.dma_start(out=zb[1:2, :], in_=v_out_b.rearrange("(o n) -> o n", o=1))
        nc.scalar.dma_start(out=zrow[0:1, :], in_=mlp_b1.rearrange("(o n) -> o n", o=1))
        load_proj(h_out_w, "hw")
        load_ctx(0)
        load_proj(v_out_w, "vw")
        load_ctx(1)
        w1_raw = raw.tile([P, 4 * 2 * E], BF16, name="w1_raw")
        nc.sync.dma_start(out=w1_raw[:].rearrange("p (j k) -> p j k", j=4), in_=mlp_w1.rearrange("(j p) k -> p j k", p=P))
        raw_tiles["w1a"] = (w1_raw[:].bitcast(F32), 512, 0)
        raw_tiles["w1b"] = (w1_raw[:].bitcast(F32), 512, 256)
        for j in range(2, N_UNITS):
            load_ctx(j)

        st = {}

        def bank():
            b = psum.tile([P, E], F32, tag="ps", name="bank")
            return b

        def transpose(n, half):
            words, row_words, first = raw_tiles[n]
            b = bank()
            for jj in range(2):
                for u in range(2):
                    start = (2 * half + jj) * row_words + first + u
                    nc.tensor.transpose(
                        b[:, u * 256 + jj * P : u * 256 + (jj + 1) * P], words[:, start : start + 2 * P - 1 : 2], ident[:]
                    )
            st["T", n, half] = b

        def exit_t(n, half, on_vector=False):
            if half == 0:
                grp = grp_pool.tile([P, 4 * E], BF16, align_bytes=64, name="grp")
                st["grp", n] = grp
            dst = st["grp", n][:].bitcast(F32)[:, half * E : (half + 1) * E].rearrange("p (r u) -> p r u", u=2)
            src = st["T", n, half][:].rearrange("p (u r) -> p r u", u=2)
            if on_vector:
                nc.vector.tensor_copy(out=dst, in_=src)
            else:
                nc.scalar.copy(out=dst, in_=src)

        def quantise(n):
            if n[0] == "x":
                codes = xq.tile([P, E], U32, align_bytes=64, name="xc")
                scales = xq.tile([P, E], U8, align_bytes=64, name="xs")
            else:
                codes = wq.tile([P, E], U32, name=n + "_c", align_bytes=64)
                scales = wq.tile([P, E], U8, name=n + "_s", align_bytes=64)
            nc.vector.quantize_mx(out=codes[:].bitcast(FP8X4), scales=scales[:], in_=st["grp", n][:])
            st["q", n] = (codes, scales)

        def biases():
            b = bank()
            zw = zb[:].bitcast(F32)
            for u in range(2):
                nc.tensor.transpose(b[:, u * P : (u + 1) * P], zw[:, u : u + 2 * P - 1 : 2], ident[:])
            bias8 = consts.tile([P, 8], F32, name="bias8")
            nc.vector.tensor_copy(
                out=bias8[:].rearrange("p (s u e) -> p u s e", s=2, u=2),
                in_=b[:].bitcast(BF16)[:, 0 : 4 * P].rearrange("p (u x) -> p u x", u=2)[:, :, 0:4].rearrange("p u (s e) -> p u s e", s=2),
            )
            st["bias8"] = bias8
            acc = bank()
            nc.tensor.matmul(out=acc[:], lhsT=ones[:], rhs=zrow[:], start=True, stop=True)
            b1_bc = consts.tile([P, E], F32, name="b1_bc")
            nc.vector.tensor_copy(out=b1_bc[:], in_=acc[:])
            st["b1"] = b1_bc

        def stage1(j):
            wc, ws = st["q", "hw" if j % 2 == 0 else "vw"]
            xc, xs = st["q", "x%d" % j]
            for t in range(4):
                b = bank()
                nc.tensor.matmul_mx(
                    out=b[:],
                    lhsT=wc[:, t * P : (t + 1) * P].bitcast(FP8X4),
                    lhsT_scale=ws[:, t * P : (t + 1) * P],
                    rhs=xc[:].bitcast(FP8X4),
                    rhs_scale=xs[:],
                    start=True,
                    stop=True,
                )
                st["M", j, t] = b

        def exit_1(j, t, on_vector=False):
            if t == 0:
                planar = pl_pool.tile([P, 4 * CHUNK], BF16, name="planar")
                st["planar", j] = planar
            dst = st["planar", j][:, t * CHUNK : (t + 1) * CHUNK]
            i = 4 * (j % 2) + t
            b = st["bias8"][:, i : i + 1]
            if on_vector:
                nc.vector.tensor_scalar_add(out=dst, in0=st["M", j, t][:], scalar1=b)
            else:
                nc.scalar.activation(out=dst, in_=st["M", j, t][:], func=ACT.Identity, bias=b, scale=1.0)

        def regroup(j):
            g2 = g2_pool.tile([P, 4 * CHUNK], BF16, align_bytes=64, name="g2")
            nc.vector.tensor_copy(
                out=g2[:].rearrange("p (c h i t) -> p h c t i", h=2, i=4, t=4),
                in_=st["planar", j][:].rearrange("p (t c h i) -> p h c t i", t=4, h=2, i=4),
            )
            st["g2", j] = g2

        def quantise2(j):
            cc = cq.tile([P, CHUNK], U32, align_bytes=64, name="cc")
            cs = cq.tile([P, CHUNK], U8, align_bytes=64, name="cs")
            nc.vector.quantize_mx(out=cc[:].bitcast(FP8X4), scales=cs[:], in_=st["g2", j][:])
            st["c", j] = (cc, cs)

        def stage2(p, i):
            c = p // 2
            a = 2 * (p % 2) + i
            b = bank()
            for g in range(2):
                cc, cs = st["c", 2 * c + g]
                mc, ms = st["q", "w1a" if g == 0 else "w1b"]
                nc.tensor.matmul_mx(
                    out=b[:],
                    lhsT=cc[:, a * P : (a + 1) * P].bitcast(FP8X4),
                    lhsT_scale=cs[:, a * P : (a + 1) * P],
                    rhs=mc[:].bitcast(FP8X4),
                    rhs_scale=ms[:],
                    start=(g == 0),
                    stop=(g == 1),
                )
            st["N", p, i] = b

        def add_b1(p, i):
            if i == 0:
                ob = ob_pool.tile([P, 2 * E], F32, name="ob")
                st["ob", p] = ob
            nc.vector.tensor_tensor(
                out=st["ob", p][:, i * E : (i + 1) * E], in0=st["N", p, i][:], in1=st["b1"][:], op=ALU.add
            )

        def relu(p, i, scalar):
            span = st["ob", p][:, i * E : (i + 1) * E]
            if scalar:
                nc.scalar.activation(out=span, in_=span, func=ACT.Relu)
            else:
                nc.vector.tensor_scalar_max(out=span, in0=span, scalar1=0.0)

        def scalar_relu_step(p):
            if p < DEFERRED_FROM:
                return p + S2_LAG + 2
            return max(N_UNITS - 1, p + S2_LAG + 1)

        def store(p, tiles):
            c = p // 2
            rows = of[c * CHUNK : (c + 1) * CHUNK, :].rearrange("(p a) f -> p a f", a=4)
            first = 2 * (p % 2)
            lo, hi = tiles[0], tiles[-1] + 1
            nc.sync.dma_start(
                out=rows[:, first + lo : first + hi, :],
                in_=st["ob", p][:, lo * E : hi * E].rearrange("p (a f) -> p a f", a=hi - lo),
            )

        def unit(m):
            return 0 <= m < N_UNITS

        def pair_on_vector(p):
            return p % 3 != 0 and p < DEFERRED_FROM

        for n in ("hw", "x0"):
            transpose(n, 0)
            transpose(n, 1)
        exit_t("hw", 0)
        exit_t("hw", 1, True)
        quantise("hw")
        exit_t("x0", 0)
        exit_t("x0", 1)
        biases()
        quantise("x0")
        for n in ("vw", "x1"):
            transpose(n, 0)
            transpose(n, 1)
            exit_t(n, 0)
            exit_t(n, 1, n == "vw")
            quantise(n)

        for m in range(N_UNITS + 5):
            x = "x%d" % (m + 2)
            p = m - S2_LAG
            if unit(m):
                stage1(m)
                for t in range(4):
                    exit_1(m, t, m == 1 and t == 3)
            if m == 0:
                for n in ("w1a", "w1b"):
                    for half in range(2):
                        transpose(n, half)
                        exit_t(n, half, n == "w1a")
            if unit(m + 2):
                for half in range(2):
                    transpose(x, half)
                    exit_t(x, half, m == 1 and half == 1)
            if unit(p):
                stage2(p, 0)
                stage2(p, 1)
            for q in range(N_UNITS):
                if scalar_relu_step(q) == m and not pair_on_vector(q):
                    if q < DEFERRED_FROM:
                        span = st["ob", q][:]
                        nc.scalar.activation(out=span, in_=span, func=ACT.Relu)
                        store(q, (0, 1))
                    else:
                        for i in range(2):
                            relu(q, i, True)
                            store(q, (i,))
            if unit(p):
                add_b1(p, 0)
            if unit(m):
                regroup(m)
            if unit(p):
                add_b1(p, 1)
            if m == 0:
                quantise("w1a")
                quantise("w1b")
            if unit(m + 2):
                quantise(x)
            if unit(p - 1) and pair_on_vector(p - 1):
                span = st["ob", p - 1][:]
                nc.vector.tensor_scalar_max(out=span, in0=span, scalar1=0.0)
                store(p - 1, (0, 1))
            if unit(m):
                quantise2(m)
